import numpy as np
import ml_dtypes


def mxq(x, axis, fmt="e4m3"):
    dtype, down = {"e4m3": (ml_dtypes.float8_e4m3fn, 7), "e5m2": (ml_dtypes.float8_e5m2, 14)}[fmt]
    v = np.moveaxis(np.asarray(x, np.float32).astype(ml_dtypes.bfloat16).astype(np.float64), axis, -1)
    blocks = v.reshape(v.shape[:-1] + (-1, 32))
    amax = np.abs(blocks).max(-1, keepdims=True)
    byte = np.maximum(np.where(amax > 0, np.frexp(amax)[1] - 1 + 127, 0) - down, 1)
    scale = np.exp2(byte - 127.0)
    codes = (blocks / scale).astype(np.float32).astype(dtype).astype(np.float64)
    return np.moveaxis((codes * scale).reshape(v.shape), -1, axis)


WIDE = False


def mx_kscale(k):
    if not WIDE:
        return np.ones(k)
    levels = np.array([10, -10, 5, -5, 0])
    if k % 512:
        return np.exp2(np.random.permutation(np.resize(levels, k // 32))).repeat(32)
    a = np.empty((k // 512, 16))
    for p in range(k // 512):
        a[p, :8] = np.random.permutation(np.resize(levels, 8))
        for g in range(8):
            far = levels[np.abs(levels - a[p, g]) >= 10]
            a[p, g + 8] = far[np.random.randint(len(far))]
    return np.exp2(a.ravel()).repeat(32)


BF16 = ml_dtypes.bfloat16


def bf(x):
    return np.asarray(x, np.float32).astype(BF16)


def f64(x):
    return np.asarray(x).astype(np.float64)


B, C, T, P, N, D = 256, 16, 512, 128, 4, 512
L = T // P
G = L // N


def setup_inputs():
    s = mx_kscale(D)
    u = mx_kscale(P * N)
    un = u.reshape(P, N).T
    ut = np.tile(u, G)
    return {'h_enc': bf(np.random.standard_normal((N, B, C, G, D)) * 0.7 * s),
            'dec_W': bf(np.random.standard_normal((N, D, P)) / np.sqrt(D) / s[None, :, None] * un[:, None, :]),
            'dec_b': bf(np.random.standard_normal((N, P)) * 0.2 * un),
            'map_W': bf(np.random.standard_normal((T, T)) / np.sqrt(T) / ut[:, None]),
            'map_b': bf(np.random.standard_normal(T) * 0.2)}


def reference(h_enc, dec_W, dec_b, map_W, map_b):
    h = f64(h_enc).reshape(N, B * C * G, D)
    r = (mxq(h, 2, 'e4m3') @ mxq(f64(dec_W), 1, 'e4m3')) + f64(dec_b)[:, None, :]
    r = r.reshape(N, B, C, G * P)
    x_rec = np.moveaxis(r, 0, -1).reshape(B * C, T)
    y_hat = (mxq(x_rec, 1, 'e4m3') @ mxq(f64(map_W), 0, 'e4m3')) + f64(map_b)
    return y_hat.reshape(B, C, T)

@@ -1,0 +1,314 @@
+from contextlib import ExitStack
+
+import concourse.mybir as mybir
+from concourse.masks import make_identity
+
+F32 = mybir.dt.float32
+BF16 = mybir.dt.bfloat16
+U32 = mybir.dt.uint32
+U8 = mybir.dt.uint8
+FP8X4 = mybir.dt.float8_e4m3fn_x4
+IDENTITY = mybir.ActivationFunctionType.Identity
+ADD = mybir.AluOpType.add
+MULT = mybir.AluOpType.mult
+
+P = 128
+MODELS = 4
+ROWS = 4096
+D = 512
+T = 512
+JB = 4
+MACRO = P * JB
+N_MACRO = ROWS // MACRO
+H_BUFS = 12
+PINNED = False
+HX_ON_VECTOR = ()
+GROUPS = [(m, 0, JB) for m in range(N_MACRO)]
+N_GROUPS = len(GROUPS)
+UNITS = N_GROUPS * MODELS
+
+FLOPS = 2 * MODELS * ROWS * D * P + 2 * ROWS * T * T
+
+
+def tile_model_pb_t_kernel(tc, h_enc, dec_W, dec_b, map_W, map_b, out):
+    nc = tc.nc
+    h = h_enc.rearrange("n b c g d -> n (b c g) d")
+    y = out.rearrange("b c s -> (b c) s")
+
+    with ExitStack() as ctx:
+        const = ctx.enter_context(tc.tile_pool(name="const", bufs=1))
+        hpool = ctx.enter_context(tc.tile_pool(name="hpool", bufs=H_BUFS))
+        gpool = ctx.enter_context(tc.tile_pool(name="gpool", bufs=4))
+        xpool = ctx.enter_context(tc.tile_pool(name="xpool", bufs=2))
+        opool = ctx.enter_context(tc.tile_pool(name="opool", bufs=3))
+        tp_ps = ctx.enter_context(tc.psum_pool(name="tp_ps", bufs=4))
+        s1_ps = ctx.enter_context(tc.psum_pool(name="s1_ps", bufs=2))
+        s2_ps = ctx.enter_context(tc.psum_pool(name="s2_ps", bufs=2))
+        if PINNED:
+            ctx.enter_context(tc.manual_schedule())
+
+        h_tiles = {}
+        tp_tiles = {}
+        hg_tiles = {}
+        hq_tiles = {}
+        s1_tiles = {}
+        xp_tiles = {}
+        xg_tiles = {}
+        xq_tiles = {}
+        s2_tiles = {}
+        o_tiles = {}
+
+        db_bf = const.tile([P, P], BF16, name="db_bf")
+        db_f = const.tile([P, P], F32, name="db_f")
+        bz = const.tile([P, T], BF16, name="bz")
+        zero = const.tile([P, 1], F32, name="zero")
+        warm = const.tile([P, 1], F32, name="warm")
+        ones = const.tile([P, P], BF16, name="ones")
+        ident = const.tile([P, P], F32, name="ident")
+        dwr = const.tile([P, MODELS, 4, P], BF16, name="dwr")
+        dwg = const.tile([P, MODELS, P, 4], BF16, name="dwg", align_bytes=64)
+        dwc = const.tile([P, MODELS * P], U32, name="dwc", align_bytes=64)
+        dws = const.tile([P, MODELS * P], U8, name="dws", align_bytes=64)
+        mwr = const.tile([P, 4, T], BF16, name="mwr")
+        mwg = const.tile([P, T, 4], BF16, name="mwg", align_bytes=64)
+        mwc = const.tile([P, T], U32, name="mwc", align_bytes=64)
+        mws = const.tile([P, T], U8, name="mws", align_bytes=64)
+        decb = const.tile([P, MODELS], F32, name="decb")
+        mapb = const.tile([P, T], F32, name="mapb")
+
+        def load_unit(k):
+            g, n = divmod(k, MODELS)
+            m, j0, nj = GROUPS[g]
+            hu = hpool.tile([P, nj * D], BF16, name="hu", tag="hu")
+            rows = h[n, m * MACRO : (m + 1) * MACRO, :].rearrange("(p j) d -> p j d", j=JB)
+            nc.sync.dma_start(
+                out=hu[:].rearrange("p (j d) -> p j d", j=nj), in_=rows[:, j0 : j0 + nj, :]
+            )
+            h_tiles[k] = hu
+
+        def load_dec_w(n):
+            nc.sync.dma_start(
+                out=dwr[:, n, :, :].rearrange("q t c -> q (t c)"),
+                in_=dec_W[n, :, :].rearrange("(q t) c -> q (t c)", t=4),
+            )
+
+        def load_map_w():
+            nc.sync.dma_start(
+                out=mwr[:].rearrange("p j s -> p (j s)"),
+                in_=map_W.rearrange("(p j) s -> p (j s)", j=4),
+            )
+
+        def prep_dec_w(n):
+            nc.gpsimd.tensor_scalar(
+                out=dwg[:, n, :, :],
+                in0=dwr[:, n, :, :].rearrange("q t c -> q c t"),
+                scalar1=1.0,
+                scalar2=0.0,
+                op0=MULT,
+                op1=ADD,
+            )
+            nc.vector.quantize_mx(
+                out=dwc[:, n * P : (n + 1) * P].bitcast(FP8X4),
+                scales=dws[:, n * P : (n + 1) * P],
+                in_=dwg[:, n, :, :].rearrange("q c t -> q (c t)"),
+            )
+
+        def prep_map_w():
+            nc.gpsimd.tensor_scalar(
+                out=mwg[:],
+                in0=mwr[:].rearrange("p j s -> p s j"),
+                scalar1=1.0,
+                scalar2=0.0,
+                op0=MULT,
+                op1=ADD,
+            )
+            nc.vector.quantize_mx(
+                out=mwc[:].bitcast(FP8X4),
+                scales=mws[:],
+                in_=mwg[:].rearrange("p s j -> p (s j)"),
+            )
+
+        def transposes(k):
+            nj = GROUPS[k // MODELS][2]
+            huf = h_tiles[k][:].bitcast(F32)
+            banks = []
+            for b in range(nj // 2):
+                tp = tp_ps.tile([P, 2, 2, P], F32, name="tp", tag="tp")
+                for a in range(2):
+                    for u in range(2):
+                        c0 = (2 * b + a) * (D // 2)
+                        nc.tensor.transpose(
+                            out=tp[:, a, u, :],
+                            in_=huf[:, c0 + u : c0 + D // 2 : 2],
+                            identity=ident[:],
+                        )
+                banks.append(tp)
+            tp_tiles[k] = banks
+
+        def h_exit(k):
+            nj = GROUPS[k // MODELS][2]
+            hg = gpool.tile([P, nj * D], BF16, name="hg", tag="hg", align_bytes=64)
+            hgf = hg[:].bitcast(F32).rearrange("q (j r u) -> q j r u", j=nj, u=2)
+            for b in range(nj // 2):
+                src = tp_tiles[k][b][:].rearrange("q a u r -> q a r u")
+                if b == 1 and k in HX_ON_VECTOR:
+                    nc.vector.tensor_copy(out=hgf[:, 2 * b : 2 * b + 2, :, :], in_=src)
+                else:
+                    nc.scalar.copy(out=hgf[:, 2 * b : 2 * b + 2, :, :], in_=src)
+            hg_tiles[k] = hg
+
+        def h_quant(k):
+            w = GROUPS[k // MODELS][2] * P
+            hc = gpool.tile([P, w], U32, name="hc", tag="hc", align_bytes=64)
+            hs = gpool.tile([P, w], U8, name="hs", tag="hs", align_bytes=64)
+            nc.vector.quantize_mx(out=hc[:].bitcast(FP8X4), scales=hs[:], in_=hg_tiles[k][:])
+            hq_tiles[k] = (hc, hs)
+
+        def stage1(k):
+            g, n = divmod(k, MODELS)
+            w = GROUPS[g][2] * P
+            hc, hs = hq_tiles[k]
+            s1 = s1_ps.tile([P, w], F32, name="s1", tag="s1")
+            nc.tensor.matmul_mx(
+                out=s1[:],
+                lhsT=dwc[:, n * P : (n + 1) * P].bitcast(FP8X4),
+                lhsT_scale=dws[:, n * P : (n + 1) * P],
+                rhs=hc[:].bitcast(FP8X4),
+                rhs_scale=hs[:],
+                start=True,
+                stop=True,
+            )
+            s1_tiles[k] = s1
+
+        def s1_exit(k):
+            g, n = divmod(k, MODELS)
+            w = GROUPS[g][2] * P
+            if n == 0:
+                xp_tiles[g] = xpool.tile([P, MODELS, w], BF16, name="xp", tag="xp")
+            nc.scalar.activation(
+                out=xp_tiles[g][:, n, :],
+                in_=s1_tiles[k][:],
+                func=IDENTITY,
+                bias=decb[:, n : n + 1],
+                scale=1.0,
+            )
+
+        def x_group(g, i):
+            w = GROUPS[g][2] * P
+            if i == 0:
+                xg_tiles[g] = xpool.tile(
+                    [P, w, MODELS], BF16, name="xg", tag="xg", align_bytes=64
+                )
+            c0 = i * 2 * P
+            c1 = c0 + 2 * P
+            dst = xg_tiles[g][:, c0:c1, :].rearrange("p (c i) t -> p c t i", i=4)
+            src = xp_tiles[g][:, :, c0:c1].rearrange("p t (c i) -> p c t i", i=4)
+            if g == N_GROUPS - 1:
+                nc.scalar.copy(out=dst, in_=src)
+            else:
+                nc.vector.tensor_copy(out=dst, in_=src)
+
+        def x_quant(g, i):
+            w = GROUPS[g][2] * P
+            if i == 0:
+                xc = xpool.tile([P, w], U32, name="xc", tag="xc", align_bytes=64)
+                xs = xpool.tile([P, w], U8, name="xs", tag="xs", align_bytes=64)
+                xq_tiles[g] = (xc, xs)
+            xc, xs = xq_tiles[g]
+            c0 = i * 2 * P
+            c1 = c0 + 2 * P
+            nc.vector.quantize_mx(
+                out=xc[:, c0:c1].bitcast(FP8X4),
+                scales=xs[:, c0:c1],
+                in_=xg_tiles[g][:, c0:c1, :].rearrange("p c t -> p (c t)"),
+            )
+
+        def stage2(g, j):
+            xc, xs = xq_tiles[g]
+            s2 = s2_ps.tile([P, T], F32, name="s2", tag="s2")
+            nc.tensor.matmul_mx(
+                out=s2[:],
+                lhsT=xc[:, j * P : (j + 1) * P].bitcast(FP8X4),
+                lhsT_scale=xs[:, j * P : (j + 1) * P],
+                rhs=mwc[:].bitcast(FP8X4),
+                rhs_scale=mws[:],
+                start=True,
+                stop=True,
+            )
+            s2_tiles[(g, j)] = s2
+
+        def s2_exit(g, j):
+            if j == 0:
+                o_tiles[g] = opool.tile([P, GROUPS[g][2], T], F32, name="ot", tag="ot")
+            nc.vector.tensor_tensor(
+                out=o_tiles[g][:, j, :], in0=s2_tiles[(g, j)][:], in1=mapb[:], op=ADD
+            )
+
+        def store(g, a, b):
+            m, j0, nj = GROUPS[g]
+            rows = y[m * MACRO : (m + 1) * MACRO, :].rearrange("(r j) s -> r j s", j=JB)
+            nc.sync.dma_start(out=rows[:, j0 + a : j0 + b, :], in_=o_tiles[g][:, a:b, :])
+
+        with tc.manual_schedule():
+            nc.vector.memset(db_bf[:], 0.0)
+            nc.scalar.dma_start(out=db_bf[0:MODELS, :], in_=dec_b)
+            nc.vector.memset(bz[:], 0.0)
+            nc.scalar.dma_start(out=bz[0:1, :], in_=map_b.rearrange("(o s) -> o s", o=1))
+            nc.vector.memset(zero[:], 0.0)
+            nc.scalar.activation(out=warm[:], in_=zero[:], func=IDENTITY)
+            nc.vector.memset(ones[:], 1.0)
+            make_identity(nc, ident[:])
+            for k in range(H_BUFS):
+                load_unit(k)
+                if k < MODELS:
+                    load_dec_w(k)
+                if k == 5:
+                    load_map_w()
+            nc.vector.tensor_copy(out=db_f[:], in_=db_bf[:])
+            transposes(0)
+            db_ps = s1_ps.tile([P, P], F32, name="db_ps", tag="s1")
+            nc.tensor.transpose(out=db_ps[:], in_=db_f[:], identity=ident[:])
+            transposes(1)
+            mb_ps = s2_ps.tile([P, T], F32, name="mb_ps", tag="s2")
+            nc.tensor.matmul(out=mb_ps[:], lhsT=ones[:], rhs=bz[:], start=True, stop=True)
+            h_exit(0)
+            nc.scalar.copy(out=decb[:], in_=db_ps[:, 0:MODELS])
+            nc.scalar.copy(out=mapb[:], in_=mb_ps[:])
+
+        for k in range(UNITS + 11):
+            if 1 <= k and k + 1 < UNITS:
+                transposes(k + 1)
+            if k + H_BUFS < UNITS:
+                load_unit(k + H_BUFS)
+            if k < MODELS:
+                prep_dec_w(k)
+            if 0 <= k - 1 < UNITS:
+                h_quant(k - 1)
+            if 1 <= k < UNITS:
+                h_exit(k)
+            for g in range(N_GROUPS):
+                for i in range(GROUPS[g][2] // 2):
+                    if k == MODELS * g + 7 + i:
+                        x_group(g, i)
+            if k == 6:
+                prep_map_w()
+            if 0 <= k - 2 < UNITS:
+                stage1(k - 2)
+            if 0 <= k - 3 < UNITS:
+                s1_exit(k - 3)
+            for g in range(N_GROUPS):
+                for i in range(GROUPS[g][2] // 2):
+                    if k == MODELS * g + 8 + i:
+                        stage2(g, 2 * i)
+                        stage2(g, 2 * i + 1)
+                    if k == MODELS * g + 9 + i:
+                        s2_exit(g, 2 * i)
+                        if g == N_GROUPS - 1:
+                            store(g, 2 * i, 2 * i + 1)
+                        s2_exit(g, 2 * i + 1)
+                        if g == N_GROUPS - 1:
+                            store(g, 2 * i + 1, 2 * i + 2)
+                        elif i == GROUPS[g][2] // 2 - 1:
+                            store(g, 0, GROUPS[g][2])
+                    if k == MODELS * g + 7 + i:
+                        x_quant(g, i)

@@ -22,10 +22,10 @@ MACRO = P * JB
 N_MACRO = ROWS // MACRO
 H_BUFS = 12
 PINNED = False
-HX_ON_VECTOR = ()
 GROUPS = [(m, 0, JB) for m in range(N_MACRO)]
 N_GROUPS = len(GROUPS)
 UNITS = N_GROUPS * MODELS
+FINE = (N_GROUPS - 1,)
 
 FLOPS = 2 * MODELS * ROWS * D * P + 2 * ROWS * T * T
 
@@ -128,33 +128,37 @@ def tile_model_pb_t_kernel(tc, h_enc, dec_W, dec_b, map_W, map_b, out):
                 in_=mwg[:].rearrange("p s j -> p (s j)"),
             )
 
+        def segment(k, b, a):
+            g, n = divmod(k, MODELS)
+            if g not in FINE:
+                j = 2 * b + a
+                return h_tiles[k][:, j * D : (j + 1) * D].bitcast(F32)
+            i, c = divmod(n, 2)
+            j = 2 * i + a
+            return h_tiles[g * MODELS + 2 * c + b][:, j * D : (j + 1) * D].bitcast(F32)
+
         def transposes(k):
-            nj = GROUPS[k // MODELS][2]
-            huf = h_tiles[k][:].bitcast(F32)
             banks = []
-            for b in range(nj // 2):
+            for b in range(2):
                 tp = tp_ps.tile([P, 2, 2, P], F32, name="tp", tag="tp")
                 for a in range(2):
                     for u in range(2):
-                        c0 = (2 * b + a) * (D // 2)
                         nc.tensor.transpose(
                             out=tp[:, a, u, :],
-                            in_=huf[:, c0 + u : c0 + D // 2 : 2],
+                            in_=segment(k, b, a)[:, u : D // 2 : 2],
                             identity=ident[:],
                         )
                 banks.append(tp)
             tp_tiles[k] = banks
 
         def h_exit(k):
-            nj = GROUPS[k // MODELS][2]
-            hg = gpool.tile([P, nj * D], BF16, name="hg", tag="hg", align_bytes=64)
-            hgf = hg[:].bitcast(F32).rearrange("q (j r u) -> q j r u", j=nj, u=2)
-            for b in range(nj // 2):
-                src = tp_tiles[k][b][:].rearrange("q a u r -> q a r u")
-                if b == 1 and k in HX_ON_VECTOR:
-                    nc.vector.tensor_copy(out=hgf[:, 2 * b : 2 * b + 2, :, :], in_=src)
-                else:
-                    nc.scalar.copy(out=hgf[:, 2 * b : 2 * b + 2, :, :], in_=src)
+            hg = gpool.tile([P, JB * D], BF16, name="hg", tag="hg", align_bytes=64)
+            hgf = hg[:].bitcast(F32).rearrange("q (j r u) -> q j r u", j=JB, u=2)
+            for b in range(2):
+                nc.scalar.copy(
+                    out=hgf[:, 2 * b : 2 * b + 2, :, :],
+                    in_=tp_tiles[k][b][:].rearrange("q a u r -> q a r u"),
+                )
             hg_tiles[k] = hg
 
         def h_quant(k):
@@ -164,34 +168,42 @@ def tile_model_pb_t_kernel(tc, h_enc, dec_W, dec_b, map_W, map_b, out):
             nc.vector.quantize_mx(out=hc[:].bitcast(FP8X4), scales=hs[:], in_=hg_tiles[k][:])
             hq_tiles[k] = (hc, hs)
 
-        def stage1(k):
+        def parts(k):
             g, n = divmod(k, MODELS)
-            w = GROUPS[g][2] * P
+            if g not in FINE:
+                return [(n, 0, MACRO, 0)]
+            i, c = divmod(n, 2)
+            w = MACRO // 2
+            return [(2 * c + b, i * w, (i + 1) * w, b * w) for b in range(2)]
+
+        def stage1(k):
             hc, hs = hq_tiles[k]
-            s1 = s1_ps.tile([P, w], F32, name="s1", tag="s1")
-            nc.tensor.matmul_mx(
-                out=s1[:],
-                lhsT=dwc[:, n * P : (n + 1) * P].bitcast(FP8X4),
-                lhsT_scale=dws[:, n * P : (n + 1) * P],
-                rhs=hc[:].bitcast(FP8X4),
-                rhs_scale=hs[:],
-                start=True,
-                stop=True,
-            )
+            s1 = s1_ps.tile([P, MACRO], F32, name="s1", tag="s1")
+            for n, r0, r1, c0 in parts(k):
+                c1 = c0 + r1 - r0
+                nc.tensor.matmul_mx(
+                    out=s1[:, c0:c1],
+                    lhsT=dwc[:, n * P : (n + 1) * P].bitcast(FP8X4),
+                    lhsT_scale=dws[:, n * P : (n + 1) * P],
+                    rhs=hc[:, c0:c1].bitcast(FP8X4),
+                    rhs_scale=hs[:, c0:c1],
+                    start=True,
+                    stop=True,
+                )
             s1_tiles[k] = s1
 
         def s1_exit(k):
             g, n = divmod(k, MODELS)
-            w = GROUPS[g][2] * P
             if n == 0:
-                xp_tiles[g] = xpool.tile([P, MODELS, w], BF16, name="xp", tag="xp")
-            nc.scalar.activation(
-                out=xp_tiles[g][:, n, :],
-                in_=s1_tiles[k][:],
-                func=IDENTITY,
-                bias=decb[:, n : n + 1],
-                scale=1.0,
-            )
+                xp_tiles[g] = xpool.tile([P, MODELS, MACRO], BF16, name="xp", tag="xp")
+            for n, r0, r1, c0 in parts(k):
+                nc.scalar.activation(
+                    out=xp_tiles[g][:, n, r0:r1],
+                    in_=s1_tiles[k][:, c0 : c0 + r1 - r0],
+                    func=IDENTITY,
+                    bias=decb[:, n : n + 1],
+                    scale=1.0,
+                )
 
         def x_group(g, i):
             w = GROUPS[g][2] * P
@@ -249,6 +261,9 @@ def tile_model_pb_t_kernel(tc, h_enc, dec_W, dec_b, map_W, map_b, out):
             rows = y[m * MACRO : (m + 1) * MACRO, :].rearrange("(r j) s -> r j s", j=JB)
             nc.sync.dma_start(out=rows[:, j0 + a : j0 + b, :], in_=o_tiles[g][:, a:b, :])
 
+        def x_step(g, i):
+            return MODELS * g + (5 + 2 * i if g in FINE else 7 + i)
+
         with tc.manual_schedule():
             nc.vector.memset(db_bf[:], 0.0)
             nc.scalar.dma_start(out=db_bf[0:MODELS, :], in_=dec_b)
@@ -275,40 +290,41 @@ def tile_model_pb_t_kernel(tc, h_enc, dec_W, dec_b, map_W, map_b, out):
             nc.scalar.copy(out=decb[:], in_=db_ps[:, 0:MODELS])
             nc.scalar.copy(out=mapb[:], in_=mb_ps[:])
 
-        for k in range(UNITS + 11):
-            if 1 <= k and k + 1 < UNITS:
-                transposes(k + 1)
-            if k + H_BUFS < UNITS:
-                load_unit(k + H_BUFS)
-            if k < MODELS:
-                prep_dec_w(k)
-            if 0 <= k - 1 < UNITS:
-                h_quant(k - 1)
-            if 1 <= k < UNITS:
-                h_exit(k)
-            for g in range(N_GROUPS):
-                for i in range(GROUPS[g][2] // 2):
-                    if k == MODELS * g + 7 + i:
-                        x_group(g, i)
-            if k == 6:
-                prep_map_w()
-            if 0 <= k - 2 < UNITS:
-                stage1(k - 2)
-            if 0 <= k - 3 < UNITS:
-                s1_exit(k - 3)
-            for g in range(N_GROUPS):
-                for i in range(GROUPS[g][2] // 2):
-                    if k == MODELS * g + 8 + i:
-                        stage2(g, 2 * i)
-                        stage2(g, 2 * i + 1)
-                    if k == MODELS * g + 9 + i:
-                        s2_exit(g, 2 * i)
-                        if g == N_GROUPS - 1:
-                            store(g, 2 * i, 2 * i + 1)
-                        s2_exit(g, 2 * i + 1)
-                        if g == N_GROUPS - 1:
-                            store(g, 2 * i + 1, 2 * i + 2)
-                        elif i == GROUPS[g][2] // 2 - 1:
-                            store(g, 0, GROUPS[g][2])
-                    if k == MODELS * g + 7 + i:
-                        x_quant(g, i)
+        with tc.manual_schedule(engines={mybir.EngineType.PE}):
+            for k in range(UNITS + 11):
+                if 1 <= k and k + 1 < UNITS:
+                    transposes(k + 1)
+                if k + H_BUFS < UNITS:
+                    load_unit(k + H_BUFS)
+                if k < MODELS:
+                    prep_dec_w(k)
+                if 0 <= k - 1 < UNITS:
+                    h_quant(k - 1)
+                if 1 <= k < UNITS:
+                    h_exit(k)
+                for g in range(N_GROUPS):
+                    for i in range(2):
+                        if k == x_step(g, i):
+                            x_group(g, i)
+                if k == 6:
+                    prep_map_w()
+                if 0 <= k - 2 < UNITS:
+                    stage1(k - 2)
+                if 0 <= k - 3 < UNITS:
+                    s1_exit(k - 3)
+                for g in range(N_GROUPS):
+                    for i in range(2):
+                        if k == x_step(g, i) + 1:
+                            stage2(g, 2 * i)
+                            stage2(g, 2 * i + 1)
+                        if k == x_step(g, i) + 2:
+                            s2_exit(g, 2 * i)
+                            if g == N_GROUPS - 1:
+                                store(g, 2 * i, 2 * i + 1)
+                            s2_exit(g, 2 * i + 1)
+                            if g == N_GROUPS - 1:
+                                store(g, 2 * i + 1, 2 * i + 2)
+                            elif i == GROUPS[g][2] // 2 - 1:
+                                store(g, 0, GROUPS[g][2])
+                        if k == x_step(g, i):
+                            x_quant(g, i)

@@ -81,9 +81,12 @@ def tile_model_pb_t_kernel(tc, h_enc, dec_W, dec_b, map_W, map_b, out):
             m, j0, nj = GROUPS[g]
             hu = hpool.tile([P, nj * D], BF16, name="hu", tag="hu")
             rows = h[n, m * MACRO : (m + 1) * MACRO, :].rearrange("(p j) d -> p j d", j=JB)
-            nc.sync.dma_start(
-                out=hu[:].rearrange("p (j d) -> p j d", j=nj), in_=rows[:, j0 : j0 + nj, :]
-            )
+            w = 2 if k == 0 else nj
+            for j in range(0, nj, w):
+                nc.sync.dma_start(
+                    out=hu[:, j * D : (j + w) * D].rearrange("p (j d) -> p j d", j=w),
+                    in_=rows[:, j0 + j : j0 + j + w, :],
+                )
             h_tiles[k] = hu
 
         def load_dec_w(n):
@@ -252,9 +255,20 @@ def tile_model_pb_t_kernel(tc, h_enc, dec_W, dec_b, map_W, map_b, out):
         def s2_exit(g, j):
             if j == 0:
                 o_tiles[g] = opool.tile([P, GROUPS[g][2], T], F32, name="ot", tag="ot")
-            nc.vector.tensor_tensor(
-                out=o_tiles[g][:, j, :], in0=s2_tiles[(g, j)][:], in1=mapb[:], op=ADD
-            )
+            w = T // 2 if (g, j) == (N_GROUPS - 1, JB - 1) else T
+            for s in range(0, T, w):
+                nc.vector.tensor_tensor(
+                    out=o_tiles[g][:, j, s : s + w],
+                    in0=s2_tiles[(g, j)][:, s : s + w],
+                    in1=mapb[:, s : s + w],
+                    op=ADD,
+                )
+                if w < T:
+                    m, j0, nj = GROUPS[g]
+                    rows = y[m * MACRO : (m + 1) * MACRO, :].rearrange("(r j) s -> r j s", j=JB)
+                    nc.sync.dma_start(
+                        out=rows[:, j, s : s + w], in_=o_tiles[g][:, j, s : s + w]
+                    )
 
         def store(g, a, b):
             m, j0, nj = GROUPS[g]
@@ -288,7 +302,6 @@ def tile_model_pb_t_kernel(tc, h_enc, dec_W, dec_b, map_W, map_b, out):
             nc.tensor.matmul(out=mb_ps[:], lhsT=ones[:], rhs=bz[:], start=True, stop=True)
             h_exit(0)
             nc.scalar.copy(out=decb[:], in_=db_ps[:, 0:MODELS])
-            nc.scalar.copy(out=mapb[:], in_=mb_ps[:])
 
         with tc.manual_schedule(engines={mybir.EngineType.PE}):
             for k in range(UNITS + 11):
@@ -308,6 +321,7 @@ def tile_model_pb_t_kernel(tc, h_enc, dec_W, dec_b, map_W, map_b, out):
                             x_group(g, i)
                 if k == 6:
                     prep_map_w()
+                    nc.vector.tensor_copy(out=mapb[:], in_=mb_ps[:])
                 if 0 <= k - 2 < UNITS:
                     stage1(k - 2)
                 if 0 <= k - 3 < UNITS:
@@ -322,9 +336,9 @@ def tile_model_pb_t_kernel(tc, h_enc, dec_W, dec_b, map_W, map_b, out):
                             if g == N_GROUPS - 1:
                                 store(g, 2 * i, 2 * i + 1)
                             s2_exit(g, 2 * i + 1)
-                            if g == N_GROUPS - 1:
+                            if g == N_GROUPS - 1 and i == 0:
                                 store(g, 2 * i + 1, 2 * i + 2)
-                            elif i == GROUPS[g][2] // 2 - 1:
+                            elif g < N_GROUPS - 1 and i == 1:
                                 store(g, 0, GROUPS[g][2])
                         if k == x_step(g, i):
                             x_quant(g, i)

@@ -218,7 +218,7 @@ def tile_model_pb_t_kernel(tc, h_enc, dec_W, dec_b, map_W, map_b, out):
             c1 = c0 + 2 * P
             dst = xg_tiles[g][:, c0:c1, :].rearrange("p (c i) t -> p c t i", i=4)
             src = xp_tiles[g][:, :, c0:c1].rearrange("p t (c i) -> p c t i", i=4)
-            if g == N_GROUPS - 1:
+            if g == N_GROUPS - 1 and i == 0:
                 nc.scalar.copy(out=dst, in_=src)
             else:
                 nc.vector.tensor_copy(out=dst, in_=src)

from contextlib import ExitStack

import concourse.mybir as mybir
from concourse.masks import make_identity

F32 = mybir.dt.float32
BF16 = mybir.dt.bfloat16
U32 = mybir.dt.uint32
U8 = mybir.dt.uint8
FP8X4 = mybir.dt.float8_e4m3fn_x4
IDENTITY = mybir.ActivationFunctionType.Identity
ADD = mybir.AluOpType.add
MULT = mybir.AluOpType.mult

P = 128
MODELS = 4
ROWS = 4096
D = 512
T = 512
JB = 4
MACRO = P * JB
N_MACRO = ROWS // MACRO
H_BUFS = 12
PINNED = False
GROUPS = [(m, 0, JB) for m in range(N_MACRO)]
N_GROUPS = len(GROUPS)
UNITS = N_GROUPS * MODELS
FINE = (N_GROUPS - 1,)

FLOPS = 2 * MODELS * ROWS * D * P + 2 * ROWS * T * T


def tile_model_pb_t_kernel(tc, h_enc, dec_W, dec_b, map_W, map_b, out):
    nc = tc.nc
    h = h_enc.rearrange("n b c g d -> n (b c g) d")
    y = out.rearrange("b c s -> (b c) s")

    with ExitStack() as ctx:
        const = ctx.enter_context(tc.tile_pool(name="const", bufs=1))
        hpool = ctx.enter_context(tc.tile_pool(name="hpool", bufs=H_BUFS))
        gpool = ctx.enter_context(tc.tile_pool(name="gpool", bufs=4))
        xpool = ctx.enter_context(tc.tile_pool(name="xpool", bufs=2))
        opool = ctx.enter_context(tc.tile_pool(name="opool", bufs=3))
        tp_ps = ctx.enter_context(tc.psum_pool(name="tp_ps", bufs=4))
        s1_ps = ctx.enter_context(tc.psum_pool(name="s1_ps", bufs=2))
        s2_ps = ctx.enter_context(tc.psum_pool(name="s2_ps", bufs=2))
        if PINNED:
            ctx.enter_context(tc.manual_schedule())

        h_tiles = {}
        tp_tiles = {}
        hg_tiles = {}
        hq_tiles = {}
        s1_tiles = {}
        xp_tiles = {}
        xg_tiles = {}
        xq_tiles = {}
        s2_tiles = {}
        o_tiles = {}

        db_bf = const.tile([P, P], BF16, name="db_bf")
        db_f = const.tile([P, P], F32, name="db_f")
        bz = const.tile([P, T], BF16, name="bz")
        zero = const.tile([P, 1], F32, name="zero")
        warm = const.tile([P, 1], F32, name="warm")
        ones = const.tile([P, P], BF16, name="ones")
        ident = const.tile([P, P], F32, name="ident")
        dwr = const.tile([P, MODELS, 4, P], BF16, name="dwr")
        dwg = const.tile([P, MODELS, P, 4], BF16, name="dwg", align_bytes=64)
        dwc = const.tile([P, MODELS * P], U32, name="dwc", align_bytes=64)
        dws = const.tile([P, MODELS * P], U8, name="dws", align_bytes=64)
        mwr = const.tile([P, 4, T], BF16, name="mwr")
        mwg = const.tile([P, T, 4], BF16, name="mwg", align_bytes=64)
        mwc = const.tile([P, T], U32, name="mwc", align_bytes=64)
        mws = const.tile([P, T], U8, name="mws", align_bytes=64)
        decb = const.tile([P, MODELS], F32, name="decb")
        mapb = const.tile([P, T], F32, name="mapb")

        def load_unit(k):
            g, n = divmod(k, MODELS)
            m, j0, nj = GROUPS[g]
            hu = hpool.tile([P, nj * D], BF16, name="hu", tag="hu")
            rows = h[n, m * MACRO : (m + 1) * MACRO, :].rearrange("(p j) d -> p j d", j=JB)
            w = 2 if k == 0 else nj
            for j in range(0, nj, w):
                nc.sync.dma_start(
                    out=hu[:, j * D : (j + w) * D].rearrange("p (j d) -> p j d", j=w),
                    in_=rows[:, j0 + j : j0 + j + w, :],
                )
            h_tiles[k] = hu

        def load_dec_w(n):
            nc.sync.dma_start(
                out=dwr[:, n, :, :].rearrange("q t c -> q (t c)"),
                in_=dec_W[n, :, :].rearrange("(q t) c -> q (t c)", t=4),
            )

        def load_map_w():
            nc.sync.dma_start(
                out=mwr[:].rearrange("p j s -> p (j s)"),
                in_=map_W.rearrange("(p j) s -> p (j s)", j=4),
            )

        def prep_dec_w(n):
            nc.gpsimd.tensor_scalar(
                out=dwg[:, n, :, :],
                in0=dwr[:, n, :, :].rearrange("q t c -> q c t"),
                scalar1=1.0,
                scalar2=0.0,
                op0=MULT,
                op1=ADD,
            )
            nc.vector.quantize_mx(
                out=dwc[:, n * P : (n + 1) * P].bitcast(FP8X4),
                scales=dws[:, n * P : (n + 1) * P],
                in_=dwg[:, n, :, :].rearrange("q c t -> q (c t)"),
            )

        def prep_map_w():
            nc.gpsimd.tensor_scalar(
                out=mwg[:],
                in0=mwr[:].rearrange("p j s -> p s j"),
                scalar1=1.0,
                scalar2=0.0,
                op0=MULT,
                op1=ADD,
            )
            nc.vector.quantize_mx(
                out=mwc[:].bitcast(FP8X4),
                scales=mws[:],
                in_=mwg[:].rearrange("p s j -> p (s j)"),
            )

        def segment(k, b, a):
            g, n = divmod(k, MODELS)
            if g not in FINE:
                j = 2 * b + a
                return h_tiles[k][:, j * D : (j + 1) * D].bitcast(F32)
            i, c = divmod(n, 2)
            j = 2 * i + a
            return h_tiles[g * MODELS + 2 * c + b][:, j * D : (j + 1) * D].bitcast(F32)

        def transposes(k):
            banks = []
            for b in range(2):
                tp = tp_ps.tile([P, 2, 2, P], F32, name="tp", tag="tp")
                for a in range(2):
                    for u in range(2):
                        nc.tensor.transpose(
                            out=tp[:, a, u, :],
                            in_=segment(k, b, a)[:, u : D // 2 : 2],
                            identity=ident[:],
                        )
                banks.append(tp)
            tp_tiles[k] = banks

        def h_exit(k):
            hg = gpool.tile([P, JB * D], BF16, name="hg", tag="hg", align_bytes=64)
            hgf = hg[:].bitcast(F32).rearrange("q (j r u) -> q j r u", j=JB, u=2)
            for b in range(2):
                nc.scalar.copy(
                    out=hgf[:, 2 * b : 2 * b + 2, :, :],
                    in_=tp_tiles[k][b][:].rearrange("q a u r -> q a r u"),
                )
            hg_tiles[k] = hg

        def h_quant(k):
            w = GROUPS[k // MODELS][2] * P
            hc = gpool.tile([P, w], U32, name="hc", tag="hc", align_bytes=64)
            hs = gpool.tile([P, w], U8, name="hs", tag="hs", align_bytes=64)
            nc.vector.quantize_mx(out=hc[:].bitcast(FP8X4), scales=hs[:], in_=hg_tiles[k][:])
            hq_tiles[k] = (hc, hs)

        def parts(k):
            g, n = divmod(k, MODELS)
            if g not in FINE:
                return [(n, 0, MACRO, 0)]
            i, c = divmod(n, 2)
            w = MACRO // 2
            return [(2 * c + b, i * w, (i + 1) * w, b * w) for b in range(2)]

        def stage1(k):
            hc, hs = hq_tiles[k]
            s1 = s1_ps.tile([P, MACRO], F32, name="s1", tag="s1")
            for n, r0, r1, c0 in parts(k):
                c1 = c0 + r1 - r0
                nc.tensor.matmul_mx(
                    out=s1[:, c0:c1],
                    lhsT=dwc[:, n * P : (n + 1) * P].bitcast(FP8X4),
                    lhsT_scale=dws[:, n * P : (n + 1) * P],
                    rhs=hc[:, c0:c1].bitcast(FP8X4),
                    rhs_scale=hs[:, c0:c1],
                    start=True,
                    stop=True,
                )
            s1_tiles[k] = s1

        def s1_exit(k):
            g, n = divmod(k, MODELS)
            if n == 0:
                xp_tiles[g] = xpool.tile([P, MODELS, MACRO], BF16, name="xp", tag="xp")
            for n, r0, r1, c0 in parts(k):
                nc.scalar.activation(
                    out=xp_tiles[g][:, n, r0:r1],
                    in_=s1_tiles[k][:, c0 : c0 + r1 - r0],
                    func=IDENTITY,
                    bias=decb[:, n : n + 1],
                    scale=1.0,
                )

        def x_group(g, i):
            w = GROUPS[g][2] * P
            if i == 0:
                xg_tiles[g] = xpool.tile(
                    [P, w, MODELS], BF16, name="xg", tag="xg", align_bytes=64
                )
            c0 = i * 2 * P
            c1 = c0 + 2 * P
            dst = xg_tiles[g][:, c0:c1, :].rearrange("p (c i) t -> p c t i", i=4)
            src = xp_tiles[g][:, :, c0:c1].rearrange("p t (c i) -> p c t i", i=4)
            if g == N_GROUPS - 1 and i == 0:
                nc.scalar.copy(out=dst, in_=src)
            else:
                nc.vector.tensor_copy(out=dst, in_=src)

        def x_quant(g, i):
            w = GROUPS[g][2] * P
            if i == 0:
                xc = xpool.tile([P, w], U32, name="xc", tag="xc", align_bytes=64)
                xs = xpool.tile([P, w], U8, name="xs", tag="xs", align_bytes=64)
                xq_tiles[g] = (xc, xs)
            xc, xs = xq_tiles[g]
            c0 = i * 2 * P
            c1 = c0 + 2 * P
            nc.vector.quantize_mx(
                out=xc[:, c0:c1].bitcast(FP8X4),
                scales=xs[:, c0:c1],
                in_=xg_tiles[g][:, c0:c1, :].rearrange("p c t -> p (c t)"),
            )

        def stage2(g, j):
            xc, xs = xq_tiles[g]
            s2 = s2_ps.tile([P, T], F32, name="s2", tag="s2")
            nc.tensor.matmul_mx(
                out=s2[:],
                lhsT=xc[:, j * P : (j + 1) * P].bitcast(FP8X4),
                lhsT_scale=xs[:, j * P : (j + 1) * P],
                rhs=mwc[:].bitcast(FP8X4),
                rhs_scale=mws[:],
                start=True,
                stop=True,
            )
            s2_tiles[(g, j)] = s2

        def s2_exit(g, j):
            if j == 0:
                o_tiles[g] = opool.tile([P, GROUPS[g][2], T], F32, name="ot", tag="ot")
            w = T // 2 if (g, j) == (N_GROUPS - 1, JB - 1) else T
            for s in range(0, T, w):
                nc.vector.tensor_tensor(
                    out=o_tiles[g][:, j, s : s + w],
                    in0=s2_tiles[(g, j)][:, s : s + w],
                    in1=mapb[:, s : s + w],
                    op=ADD,
                )
                if w < T:
                    m, j0, nj = GROUPS[g]
                    rows = y[m * MACRO : (m + 1) * MACRO, :].rearrange("(r j) s -> r j s", j=JB)
                    nc.sync.dma_start(
                        out=rows[:, j, s : s + w], in_=o_tiles[g][:, j, s : s + w]
                    )

        def store(g, a, b):
            m, j0, nj = GROUPS[g]
            rows = y[m * MACRO : (m + 1) * MACRO, :].rearrange("(r j) s -> r j s", j=JB)
            nc.sync.dma_start(out=rows[:, j0 + a : j0 + b, :], in_=o_tiles[g][:, a:b, :])

        def x_step(g, i):
            return MODELS * g + (5 + 2 * i if g in FINE else 7 + i)

        with tc.manual_schedule():
            nc.vector.memset(db_bf[:], 0.0)
            nc.scalar.dma_start(out=db_bf[0:MODELS, :], in_=dec_b)
            nc.vector.memset(bz[:], 0.0)
            nc.scalar.dma_start(out=bz[0:1, :], in_=map_b.rearrange("(o s) -> o s", o=1))
            nc.vector.memset(zero[:], 0.0)
            nc.scalar.activation(out=warm[:], in_=zero[:], func=IDENTITY)
            nc.vector.memset(ones[:], 1.0)
            make_identity(nc, ident[:])
            for k in range(H_BUFS):
                load_unit(k)
                if k < MODELS:
                    load_dec_w(k)
                if k == 5:
                    load_map_w()
            nc.vector.tensor_copy(out=db_f[:], in_=db_bf[:])
            transposes(0)
            db_ps = s1_ps.tile([P, P], F32, name="db_ps", tag="s1")
            nc.tensor.transpose(out=db_ps[:], in_=db_f[:], identity=ident[:])
            transposes(1)
            mb_ps = s2_ps.tile([P, T], F32, name="mb_ps", tag="s2")
            nc.tensor.matmul(out=mb_ps[:], lhsT=ones[:], rhs=bz[:], start=True, stop=True)
            h_exit(0)
            nc.scalar.copy(out=decb[:], in_=db_ps[:, 0:MODELS])

        with tc.manual_schedule(engines={mybir.EngineType.PE}):
            for k in range(UNITS + 11):
                if 1 <= k and k + 1 < UNITS:
                    transposes(k + 1)
                if k + H_BUFS < UNITS:
                    load_unit(k + H_BUFS)
                if k < MODELS:
                    prep_dec_w(k)
                if 0 <= k - 1 < UNITS:
                    h_quant(k - 1)
                if 1 <= k < UNITS:
                    h_exit(k)
                for g in range(N_GROUPS):
                    for i in range(2):
                        if k == x_step(g, i):
                            x_group(g, i)
                if k == 6:
                    prep_map_w()
                    nc.vector.tensor_copy(out=mapb[:], in_=mb_ps[:])
                if 0 <= k - 2 < UNITS:
                    stage1(k - 2)
                if 0 <= k - 3 < UNITS:
                    s1_exit(k - 3)
                for g in range(N_GROUPS):
                    for i in range(2):
                        if k == x_step(g, i) + 1:
                            stage2(g, 2 * i)
                            stage2(g, 2 * i + 1)
                        if k == x_step(g, i) + 2:
                            s2_exit(g, 2 * i)
                            if g == N_GROUPS - 1:
                                store(g, 2 * i, 2 * i + 1)
                            s2_exit(g, 2 * i + 1)
                            if g == N_GROUPS - 1 and i == 0:
                                store(g, 2 * i + 1, 2 * i + 2)
                            elif g < N_GROUPS - 1 and i == 1:
                                store(g, 0, GROUPS[g][2])
                        if k == x_step(g, i):
                            x_quant(g, i)
